import numpy as np
import ml_dtypes


def mxq(x, axis, fmt="e4m3"):
    dtype, down = {"e4m3": (ml_dtypes.float8_e4m3fn, 7), "e5m2": (ml_dtypes.float8_e5m2, 14)}[fmt]
    v = np.moveaxis(np.asarray(x, np.float32).astype(ml_dtypes.bfloat16).astype(np.float64), axis, -1)
    blocks = v.reshape(v.shape[:-1] + (-1, 32))
    amax = np.abs(blocks).max(-1, keepdims=True)
    byte = np.maximum(np.where(amax > 0, np.frexp(amax)[1] - 1 + 127, 0) - down, 1)
    scale = np.exp2(byte - 127.0)
    codes = (blocks / scale).astype(np.float32).astype(dtype).astype(np.float64)
    return np.moveaxis((codes * scale).reshape(v.shape), -1, axis)


WIDE = False


def mx_kscale(k):
    if not WIDE:
        return np.ones(k)
    levels = np.array([10, -10, 5, -5, 0])
    a = np.random.permutation(np.resize(levels, k // 512 * 4)).reshape(k // 512, 4)
    idx = np.arange(k)
    return np.exp2(a[idx // 512, idx % 128 // 32])


BF16 = ml_dtypes.bfloat16


def bf(x):
    return np.asarray(x, np.float32).astype(BF16)


def f64(x):
    return np.asarray(x).astype(np.float64)


B, S, H, NH = 4, 256, 1024, 16
DK = H // NH
NORM_EPS = 1e-6


def elu(v):
    return np.where(v > 0.0, v, np.exp(np.minimum(v, 0.0)) - 1.0)


def setup_inputs():
    s = mx_kscale(H)
    w = 1.0 / np.sqrt(H)
    return {"hidden_states": bf(np.random.standard_normal((B, S, H)) * s),
            "Wq": bf(np.random.standard_normal((H, H)) * 1.5 * w / s[:, None]),
            "Wk": bf(np.random.standard_normal((H, H)) * 1.5 * w / s[:, None]),
            "Wv": bf(np.random.standard_normal((H, H)) * 2.0 * w / s[:, None])}


def reference(hidden_states, Wq, Wk, Wv):
    xq = mxq(f64(hidden_states), 2, "e4m3")
    q = (xq @ mxq(f64(Wq), 0, "e4m3")).reshape(B, S, NH, DK)
    k = (xq @ mxq(f64(Wk), 0, "e4m3")).reshape(B, S, NH, DK)
    v = (xq @ mxq(f64(Wv), 0, "e4m3")).reshape(B, S, NH, DK)
    q = elu(q) + 1.0
    k = elu(k) + 1.0
    qk = np.sum(q * k, axis=-1, keepdims=True)
    k_sum = np.sum(k, axis=1, keepdims=True)
    normalizer = np.sum(q * k_sum, axis=-1, keepdims=True)
    z = qk * v / (normalizer + NORM_EPS)
    return z.reshape(B, S, H)

@@ -1,0 +1,270 @@
+from contextlib import ExitStack
+
+import concourse.mybir as mybir
+from concourse.masks import make_identity
+
+F32 = mybir.dt.float32
+BF16 = mybir.dt.bfloat16
+U32 = mybir.dt.uint32
+U8 = mybir.dt.uint8
+FP8X4 = mybir.dt.float8_e4m3fn_x4
+ALU = mybir.AluOpType
+ACT = mybir.ActivationFunctionType
+
+P = 128
+PACK = 4
+K_PASS = P * PACK
+TOKENS = 1024
+SEQ = 256
+HIDDEN = 1024
+HEAD = 64
+PASSES = HIDDEN // K_PASS
+BANK = 512
+HALVES = TOKENS // BANK
+GROUPS = HIDDEN // BANK
+TILES = BANK // P
+BATCHES = BANK // SEQ
+TILE_HEADS = P // HEAD
+GROUP_HEADS = BANK // HEAD
+NORM_EPS = 1e-6
+
+FLOPS = 3 * 2 * TOKENS * HIDDEN * HIDDEN
+
+
+def tile_gatedlinearattention_pa_kernel(tc, hidden_states, Wq, Wk, Wv, out):
+    nc = tc.nc
+    x_dram = hidden_states.flatten_outer_dims()
+    out_dram = out.flatten_outer_dims()
+    weight_dram = {"q": Wq, "k": Wk, "v": Wv}
+
+    with ExitStack() as pools:
+        const = pools.enter_context(tc.tile_pool(name="const", bufs=1))
+        keep = pools.enter_context(tc.tile_pool(name="keep", bufs=1))
+        stage = pools.enter_context(tc.tile_pool(name="stage", bufs=4))
+        work = pools.enter_context(tc.tile_pool(name="work", bufs=3))
+        small = pools.enter_context(tc.tile_pool(name="small", bufs=4))
+        psum = pools.enter_context(tc.psum_pool(name="psum", bufs=2))
+
+        identity = const.tile([P, P], F32)
+        make_identity(nc, identity[:])
+        head_mask = const.tile([P, TILE_HEADS], F32)
+        nc.vector.tensor_reduce(
+            out=head_mask[:],
+            in_=identity[:].rearrange("p (j d) -> p j d", d=HEAD),
+            axis=mybir.AxisListType.X,
+            op=ALU.add,
+        )
+        warm = const.tile([P, 2], F32)
+        nc.vector.memset(warm[:], 0.0)
+        nc.scalar.activation(out=warm[:, 1:2], in_=warm[:, 0:1], func=ACT.Exp)
+
+        x_raw = {}
+
+        def load_x(half):
+            for pair in range(TILES // 2):
+                first = half * BANK + pair * 2 * P
+                raw = keep.tile([P, 2, HIDDEN], BF16, name="x_raw_%d_%d" % (half, pair))
+                nc.sync.dma_start(
+                    out=raw[:],
+                    in_=x_dram[first : first + 2 * P, :].rearrange("(i p) k -> p i k", p=P),
+                )
+                x_raw[(half, pair)] = raw
+
+        w_raw = {}
+
+        def load_w(w, group):
+            for g in range(PASSES):
+                raw = keep.tile([P, PACK, BANK], BF16, name="w_raw_%s_%d_%d" % (w, group, g))
+                nc.sync.dma_start(
+                    out=raw[:],
+                    in_=weight_dram[w][
+                        g * K_PASS : (g + 1) * K_PASS, group * BANK : (group + 1) * BANK
+                    ].rearrange("(p j) n -> p j n", j=PACK),
+                )
+                w_raw[(w, group, g)] = raw
+
+        load_x(0)
+        load_w("q", 0)
+        load_w("k", 0)
+        load_x(1)
+        load_w("v", 0)
+        load_w("q", 1)
+        load_w("k", 1)
+        load_w("v", 1)
+
+        x_codes = {}
+        x_scales = {}
+
+        def prepare_x(half):
+            grouped = keep.tile([P, PASSES * BANK * PACK], BF16, name="x_grouped_%d" % half, align_bytes=64)
+            grouped_words = grouped[:].bitcast(F32).rearrange("p (g r u) -> p g r u", g=PASSES, u=2)
+            for i in range(TILES):
+                words = x_raw[(half, i // 2)][:, i % 2, :].bitcast(F32).rearrange(
+                    "p (g w u) -> p g u w", g=PASSES, u=2
+                )
+                turned = psum.tile([P, PASSES, 2, P], F32, tag="v")
+                for g in range(PASSES):
+                    for u in range(2):
+                        nc.tensor.transpose(
+                            out=turned[:, g, u, :], in_=words[:, g, u, :], identity=identity[:]
+                        )
+                nc.scalar.copy(
+                    out=grouped_words[:, :, i * P : (i + 1) * P, :],
+                    in_=turned[:].rearrange("p g u r -> p g r u"),
+                )
+            codes = keep.tile([P, PASSES, BANK], U32, name="x_codes_%d" % half, align_bytes=64)
+            scales = keep.tile([P, PASSES, BANK], U8, name="x_scales_%d" % half, align_bytes=64)
+            for g in range(PASSES):
+                nc.vector.quantize_mx(
+                    out=codes[:, g, :].bitcast(FP8X4),
+                    scales=scales[:, g, :],
+                    in_=grouped[:, g * BANK * PACK : (g + 1) * BANK * PACK],
+                )
+            x_codes[half] = codes
+            x_scales[half] = scales
+
+        w_codes = {}
+        w_scales = {}
+        w_grouped = {}
+
+        def regroup(unit, engine_copy):
+            grouped = stage.tile([P, BANK, PACK], BF16, tag="w_grouped", name="w_grouped_%s_%d_%d" % unit, align_bytes=64)
+            engine_copy(
+                out=grouped[:].rearrange("p (c i) t -> p c t i", i=4),
+                in_=w_raw[unit][:].rearrange("p t (c i) -> p c t i", i=4),
+            )
+            w_grouped[unit] = grouped
+
+        def quantise(unit):
+            w, group, g = unit
+            if g == 0:
+                w_codes[(w, group)] = keep.tile([P, PASSES, BANK], U32, name="w_codes_%s_%d" % (w, group), align_bytes=64)
+                w_scales[(w, group)] = keep.tile([P, PASSES, BANK], U8, name="w_scales_%s_%d" % (w, group), align_bytes=64)
+            nc.vector.quantize_mx(
+                out=w_codes[(w, group)][:, g, :].bitcast(FP8X4),
+                scales=w_scales[(w, group)][:, g, :],
+                in_=w_grouped[unit][:].rearrange("p n t -> p (n t)"),
+            )
+
+        def prepare_weights(names, group):
+            for w in names:
+                regroup((w, group, 0), nc.scalar.copy)
+                regroup((w, group, 1), nc.vector.tensor_copy)
+                quantise((w, group, 0))
+                quantise((w, group, 1))
+
+        prepare_x(0)
+        prepare_weights(("q", "k"), 0)
+        prepare_x(1)
+        prepare_weights(("v",), 0)
+        prepare_weights(("q", "k", "v"), 1)
+
+        def project_transposed(w, group, t, half, tag):
+            acc = psum.tile([P, BANK], F32, tag=tag)
+            for g in range(PASSES):
+                nc.tensor.matmul_mx(
+                    out=acc[:],
+                    lhsT=w_codes[(w, group)][:, g, t * P : (t + 1) * P].bitcast(FP8X4),
+                    lhsT_scale=w_scales[(w, group)][:, g, t * P : (t + 1) * P],
+                    rhs=x_codes[half][:, g, :].bitcast(FP8X4),
+                    rhs_scale=x_scales[half][:, g, :],
+                    start=(g == 0),
+                    stop=(g == PASSES - 1),
+                )
+            return acc
+
+        def feature_round(group, half, t, sums):
+            a = project_transposed("q", group, t, half, "a")
+            c = project_transposed("k", group, t, half, "c")
+            exp_a = work.tile([P, BANK], F32)
+            relu_a = work.tile([P, BANK], F32)
+            exp_c = work.tile([P, BANK], F32)
+            relu_c = work.tile([P, BANK], F32)
+            nc.scalar.activation(out=exp_a[:], in_=a[:], func=ACT.Exp)
+            nc.scalar.activation(out=relu_a[:], in_=a[:], func=ACT.Relu)
+            nc.scalar.activation(out=exp_c[:], in_=c[:], func=ACT.Exp)
+            nc.scalar.activation(out=relu_c[:], in_=c[:], func=ACT.Relu)
+            q = work.tile([P, BANK], F32)
+            k = work.tile([P, BANK], F32)
+            k_sum = small.tile([P, BATCHES], F32)
+            nc.vector.scalar_tensor_tensor(
+                out=q[:], in0=exp_a[:], scalar=1.0, in1=relu_a[:], op0=ALU.min, op1=ALU.add
+            )
+            for b in range(BATCHES):
+                cols = slice(b * SEQ, (b + 1) * SEQ)
+                nc.vector.scalar_tensor_tensor(
+                    out=k[:, cols],
+                    in0=exp_c[:, cols],
+                    scalar=1.0,
+                    in1=relu_c[:, cols],
+                    op0=ALU.min,
+                    op1=ALU.add,
+                    accum_out=k_sum[:, b : b + 1],
+                )
+            qk = work.tile([P, BANK], F32)
+            nc.vector.tensor_tensor(out=qk[:], in0=q[:], in1=k[:], op=ALU.mult)
+            k_sum_by_head = small.tile([P, BATCHES, TILE_HEADS], F32)
+            nc.vector.tensor_tensor(
+                out=k_sum_by_head[:],
+                in0=head_mask[:].unsqueeze(1).to_broadcast([P, BATCHES, TILE_HEADS]),
+                in1=k_sum[:].unsqueeze(2).to_broadcast([P, BATCHES, TILE_HEADS]),
+                op=ALU.mult,
+            )
+            heads = slice(t * TILE_HEADS, (t + 1) * TILE_HEADS)
+            for s in range(TILES):
+                tokens = slice(s * P, (s + 1) * P)
+                nc.tensor.matmul(
+                    out=sums[:, s, 0, heads], lhsT=qk[:, tokens], rhs=head_mask[:], start=True, stop=True
+                )
+                nc.tensor.matmul(
+                    out=sums[:, s, 1, heads],
+                    lhsT=q[:, tokens],
+                    rhs=k_sum_by_head[:, s * P // SEQ, :],
+                    start=True,
+                    stop=True,
+                )
+
+        def form_ratio(sums):
+            normalizer = small.tile([P, TILES, GROUP_HEADS], F32)
+            inverse = small.tile([P, TILES, GROUP_HEADS], F32)
+            ratio = small.tile([P, TILES, GROUP_HEADS], F32)
+            nc.vector.tensor_scalar_add(out=normalizer[:], in0=sums[:, :, 1, :], scalar1=NORM_EPS)
+            nc.vector.reciprocal(out=inverse[:], in_=normalizer[:])
+            nc.vector.tensor_tensor(out=ratio[:], in0=sums[:, :, 0, :], in1=inverse[:], op=ALU.mult)
+            return ratio
+
+        def value_tile(group, half, s, ratio):
+            v = psum.tile([P, BANK], F32, tag="v")
+            for g in range(PASSES):
+                nc.tensor.matmul_mx(
+                    out=v[:],
+                    lhsT=x_codes[half][:, g, s * P : (s + 1) * P].bitcast(FP8X4),
+                    lhsT_scale=x_scales[half][:, g, s * P : (s + 1) * P],
+                    rhs=w_codes[("v", group)][:, g, :].bitcast(FP8X4),
+                    rhs_scale=w_scales[("v", group)][:, g, :],
+                    start=(g == 0),
+                    stop=(g == PASSES - 1),
+                )
+            z = work.tile([P, BANK], F32)
+            nc.vector.tensor_tensor(
+                out=z[:].rearrange("p (h d) -> p h d", d=HEAD),
+                in0=v[:].rearrange("p (h d) -> p h d", d=HEAD),
+                in1=ratio[:, s, :].unsqueeze(2).to_broadcast([P, GROUP_HEADS, HEAD]),
+                op=ALU.mult,
+            )
+            first = half * BANK + s * P
+            nc.sync.dma_start(
+                out=out_dram[first : first + P, group * BANK : (group + 1) * BANK], in_=z[:]
+            )
+
+        finished = None
+        for group in range(GROUPS):
+            for half in range(HALVES):
+                sums = psum.tile([P, TILES, 2, GROUP_HEADS], F32, tag="sums")
+                for t in range(TILES):
+                    feature_round(group, half, t, sums)
+                    if finished is not None:
+                        value_tile(finished[0], finished[1], t, finished[2])
+                finished = (group, half, form_ratio(sums))
+        for s in range(TILES):
+            value_tile(finished[0], finished[1], s, finished[2])

@@ -24,8 +24,10 @@ HALVES = TOKENS // BANK
 GROUPS = HIDDEN // BANK
 TILES = BANK // P
 BATCHES = BANK // SEQ
-TILE_HEADS = P // HEAD
 GROUP_HEADS = BANK // HEAD
+HEAD_ROWS = P // GROUP_HEADS
+ROUNDS = GROUPS * HALVES * TILES
+AHEAD = 2
 NORM_EPS = 1e-6
 
 FLOPS = 3 * 2 * TOKENS * HIDDEN * HIDDEN
@@ -43,17 +45,12 @@ def tile_gatedlinearattention_pa_kernel(tc, hidden_states, Wq, Wk, Wv, out):
         stage = pools.enter_context(tc.tile_pool(name="stage", bufs=4))
         work = pools.enter_context(tc.tile_pool(name="work", bufs=3))
         small = pools.enter_context(tc.tile_pool(name="small", bufs=4))
+        products = pools.enter_context(tc.tile_pool(name="products", bufs=2 * TILES))
         psum = pools.enter_context(tc.psum_pool(name="psum", bufs=2))
+        pools.enter_context(tc.manual_schedule())
 
         identity = const.tile([P, P], F32)
         make_identity(nc, identity[:])
-        head_mask = const.tile([P, TILE_HEADS], F32)
-        nc.vector.tensor_reduce(
-            out=head_mask[:],
-            in_=identity[:].rearrange("p (j d) -> p j d", d=HEAD),
-            axis=mybir.AxisListType.X,
-            op=ALU.add,
-        )
         warm = const.tile([P, 2], F32)
         nc.vector.memset(warm[:], 0.0)
         nc.scalar.activation(out=warm[:, 1:2], in_=warm[:, 0:1], func=ACT.Exp)
@@ -83,19 +80,21 @@ def tile_gatedlinearattention_pa_kernel(tc, hidden_states, Wq, Wk, Wv, out):
                 )
                 w_raw[(w, group, g)] = raw
 
+        later_operands = [("x", 1), ("v", 0), ("q", 1), ("k", 1), ("v", 1)]
         load_x(0)
         load_w("q", 0)
         load_w("k", 0)
-        load_x(1)
-        load_w("v", 0)
-        load_w("q", 1)
-        load_w("k", 1)
-        load_w("v", 1)
+        for name, index in later_operands:
+            if name == "x":
+                load_x(index)
+            else:
+                load_w(name, index)
 
+        x_grouped = {}
         x_codes = {}
         x_scales = {}
 
-        def prepare_x(half):
+        def turn_x(half):
             grouped = keep.tile([P, PASSES * BANK * PACK], BF16, name="x_grouped_%d" % half, align_bytes=64)
             grouped_words = grouped[:].bitcast(F32).rearrange("p (g r u) -> p g r u", g=PASSES, u=2)
             for i in range(TILES):
@@ -112,54 +111,66 @@ def tile_gatedlinearattention_pa_kernel(tc, hidden_states, Wq, Wk, Wv, out):
                     out=grouped_words[:, :, i * P : (i + 1) * P, :],
                     in_=turned[:].rearrange("p g u r -> p g r u"),
                 )
+            x_grouped[half] = grouped
+
+        def quantise_x(half):
             codes = keep.tile([P, PASSES, BANK], U32, name="x_codes_%d" % half, align_bytes=64)
             scales = keep.tile([P, PASSES, BANK], U8, name="x_scales_%d" % half, align_bytes=64)
             for g in range(PASSES):
                 nc.vector.quantize_mx(
                     out=codes[:, g, :].bitcast(FP8X4),
                     scales=scales[:, g, :],
-                    in_=grouped[:, g * BANK * PACK : (g + 1) * BANK * PACK],
+                    in_=x_grouped[half][:, g * BANK * PACK : (g + 1) * BANK * PACK],
                 )
             x_codes[half] = codes
             x_scales[half] = scales
 
+        w_grouped = {}
         w_codes = {}
         w_scales = {}
-        w_grouped = {}
 
-        def regroup(unit, engine_copy):
-            grouped = stage.tile([P, BANK, PACK], BF16, tag="w_grouped", name="w_grouped_%s_%d_%d" % unit, align_bytes=64)
-            engine_copy(
-                out=grouped[:].rearrange("p (c i) t -> p c t i", i=4),
-                in_=w_raw[unit][:].rearrange("p t (c i) -> p c t i", i=4),
-            )
-            w_grouped[unit] = grouped
+        def regroup_w(w, group):
+            order = "p (c i) t -> p c t i" if w == "v" else "p (i c) t -> p c t i"
+            for g, engine_copy in ((0, nc.scalar.copy), (1, nc.vector.tensor_copy)):
+                grouped = stage.tile([P, BANK, PACK], BF16, tag="w_grouped", name="w_grouped_%s_%d_%d" % (w, group, g), align_bytes=64)
+                engine_copy(
+                    out=grouped[:].rearrange(order, i=4),
+                    in_=w_raw[(w, group, g)][:].rearrange("p t (c i) -> p c t i", i=4),
+                )
+                w_grouped[(w, group, g)] = grouped
 
-        def quantise(unit):
-            w, group, g = unit
-            if g == 0:
-                w_codes[(w, group)] = keep.tile([P, PASSES, BANK], U32, name="w_codes_%s_%d" % (w, group), align_bytes=64)
-                w_scales[(w, group)] = keep.tile([P, PASSES, BANK], U8, name="w_scales_%s_%d" % (w, group), align_bytes=64)
-            nc.vector.quantize_mx(
-                out=w_codes[(w, group)][:, g, :].bitcast(FP8X4),
-                scales=w_scales[(w, group)][:, g, :],
-                in_=w_grouped[unit][:].rearrange("p n t -> p (n t)"),
-            )
+        def quantise_w(w, group):
+            codes = keep.tile([P, PASSES, BANK], U32, name="w_codes_%s_%d" % (w, group), align_bytes=64)
+            scales = keep.tile([P, PASSES, BANK], U8, name="w_scales_%s_%d" % (w, group), align_bytes=64)
+            for g in range(PASSES):
+                nc.vector.quantize_mx(
+                    out=codes[:, g, :].bitcast(FP8X4),
+                    scales=scales[:, g, :],
+                    in_=w_grouped[(w, group, g)][:].rearrange("p n t -> p (n t)"),
+                )
+            w_codes[(w, group)] = codes
+            w_scales[(w, group)] = scales
 
-        def prepare_weights(names, group):
-            for w in names:
-                regroup((w, group, 0), nc.scalar.copy)
-                regroup((w, group, 1), nc.vector.tensor_copy)
-                quantise((w, group, 0))
-                quantise((w, group, 1))
+        def prepare(name, index):
+            if name == "x":
+                turn_x(index)
+                quantise_x(index)
+            else:
+                regroup_w(name, index)
+                quantise_w(name, index)
 
-        prepare_x(0)
-        prepare_weights(("q", "k"), 0)
-        prepare_x(1)
-        prepare_weights(("v",), 0)
-        prepare_weights(("q", "k", "v"), 1)
+        def place(number):
+            block, tile_in_block = divmod(number, TILES)
+            group, half = divmod(block, HALVES)
+            return group, half, tile_in_block
 
-        def project_transposed(w, group, t, half, tag):
+        a_banks = {}
+        c_banks = {}
+
+        def project(r, w, banks, tag):
+            if r >= ROUNDS:
+                return
+            group, half, t = place(r)
             acc = psum.tile([P, BANK], F32, tag=tag)
             for g in range(PASSES):
                 nc.tensor.matmul_mx(
@@ -171,11 +182,15 @@ def tile_gatedlinearattention_pa_kernel(tc, hidden_states, Wq, Wk, Wv, out):
                     start=(g == 0),
                     stop=(g == PASSES - 1),
                 )
-            return acc
+            banks[r] = acc
 
-        def feature_round(group, half, t, sums):
-            a = project_transposed("q", group, t, half, "a")
-            c = project_transposed("k", group, t, half, "c")
+        q_tiles = {}
+        k_tiles = {}
+        k_sums = {}
+
+        def feature_map(r):
+            a = a_banks[r]
+            c = c_banks[r]
             exp_a = work.tile([P, BANK], F32)
             relu_a = work.tile([P, BANK], F32)
             exp_c = work.tile([P, BANK], F32)
@@ -201,39 +216,75 @@ def tile_gatedlinearattention_pa_kernel(tc, hidden_states, Wq, Wk, Wv, out):
                     op1=ALU.add,
                     accum_out=k_sum[:, b : b + 1],
                 )
-            qk = work.tile([P, BANK], F32)
-            nc.vector.tensor_tensor(out=qk[:], in0=q[:], in1=k[:], op=ALU.mult)
-            k_sum_by_head = small.tile([P, BATCHES, TILE_HEADS], F32)
-            nc.vector.tensor_tensor(
-                out=k_sum_by_head[:],
-                in0=head_mask[:].unsqueeze(1).to_broadcast([P, BATCHES, TILE_HEADS]),
-                in1=k_sum[:].unsqueeze(2).to_broadcast([P, BATCHES, TILE_HEADS]),
-                op=ALU.mult,
-            )
-            heads = slice(t * TILE_HEADS, (t + 1) * TILE_HEADS)
-            for s in range(TILES):
-                tokens = slice(s * P, (s + 1) * P)
-                nc.tensor.matmul(
-                    out=sums[:, s, 0, heads], lhsT=qk[:, tokens], rhs=head_mask[:], start=True, stop=True
-                )
-                nc.tensor.matmul(
-                    out=sums[:, s, 1, heads],
-                    lhsT=q[:, tokens],
-                    rhs=k_sum_by_head[:, s * P // SEQ, :],
-                    start=True,
-                    stop=True,
-                )
+            q_tiles[r] = q
+            k_tiles[r] = k
+            k_sums[r] = k_sum
 
-        def form_ratio(sums):
-            normalizer = small.tile([P, TILES, GROUP_HEADS], F32)
-            inverse = small.tile([P, TILES, GROUP_HEADS], F32)
+        qk_tiles = {}
+        qs_tiles = {}
+
+        def form_products(r):
+            qk = products.tile([P, BANK], F32)
+            nc.vector.tensor_tensor(out=qk[:], in0=q_tiles[r][:], in1=k_tiles[r][:], op=ALU.mult)
+            qs = products.tile([P, BANK], F32)
+            for b in range(BATCHES):
+                cols = slice(b * SEQ, (b + 1) * SEQ)
+                nc.gpsimd.tensor_scalar(
+                    out=qs[:, cols],
+                    in0=q_tiles[r][:, cols],
+                    scalar1=k_sums[r][:, b : b + 1],
+                    scalar2=0.0,
+                    op0=ALU.mult,
+                    op1=ALU.add,
+                )
+            qk_tiles[r] = qk
+            qs_tiles[r] = qs
+
+        block_sums = {}
+
+        def head_sums(block):
+            for kind, tiles in (("qk", qk_tiles), ("qs", qs_tiles)):
+                turned = psum.tile([P, TILES, P], F32, tag="sum_" + kind, name="sum_" + kind, bufs=1)
+                for s in range(TILES):
+                    for t in range(TILES):
+                        nc.tensor.matmul(
+                            out=turned[:, s, :],
+                            lhsT=tiles[block * TILES + t][:, s * P : (s + 1) * P],
+                            rhs=identity[:],
+                            is_transpose=True,
+                            start=(t == 0),
+                            stop=(t == TILES - 1),
+                        )
+                block_sums[(kind, block)] = turned
+
+        ratios = {}
+
+        def form_ratio(block):
+            totals = {}
+            for kind in ("qk", "qs"):
+                totals[kind] = small.tile([P, TILES * GROUP_HEADS], F32, name="total_" + kind)
+                nc.vector.tensor_reduce(
+                    out=totals[kind][:],
+                    in_=block_sums[(kind, block)][:].rearrange("p s (h e) -> p (s h) e", e=HEAD_ROWS),
+                    axis=mybir.AxisListType.X,
+                    op=ALU.add,
+                )
+            normalizer = small.tile([P, TILES * GROUP_HEADS], F32)
+            inverse = small.tile([P, TILES * GROUP_HEADS], F32)
             ratio = small.tile([P, TILES, GROUP_HEADS], F32)
-            nc.vector.tensor_scalar_add(out=normalizer[:], in0=sums[:, :, 1, :], scalar1=NORM_EPS)
+            nc.vector.tensor_scalar_add(out=normalizer[:], in0=totals["qs"][:], scalar1=NORM_EPS)
             nc.vector.reciprocal(out=inverse[:], in_=normalizer[:])
-            nc.vector.tensor_tensor(out=ratio[:], in0=sums[:, :, 0, :], in1=inverse[:], op=ALU.mult)
-            return ratio
+            nc.vector.tensor_tensor(
+                out=ratio[:].rearrange("p s h -> p (s h)"), in0=totals["qk"][:], in1=inverse[:], op=ALU.mult
+            )
+            ratios[block] = ratio
 
-        def value_tile(group, half, s, ratio):
+        v_banks = {}
+
+        def project_value(j):
+            if not 0 <= j < ROUNDS:
+                return
+            group, half, s = place(j)
             v = psum.tile([P, BANK], F32, tag="v")
             for g in range(PASSES):
                 nc.tensor.matmul_mx(
@@ -245,11 +296,19 @@ def tile_gatedlinearattention_pa_kernel(tc, hidden_states, Wq, Wk, Wv, out):
                     start=(g == 0),
                     stop=(g == PASSES - 1),
                 )
+            v_banks[j] = v
+
+        def scale_and_store(j):
+            if j < 0:
+                return
+            group, half, s = place(j)
+            if s == 0:
+                form_ratio(j // TILES)
             z = work.tile([P, BANK], F32)
             nc.vector.tensor_tensor(
                 out=z[:].rearrange("p (h d) -> p h d", d=HEAD),
-                in0=v[:].rearrange("p (h d) -> p h d", d=HEAD),
-                in1=ratio[:, s, :].unsqueeze(2).to_broadcast([P, GROUP_HEADS, HEAD]),
+                in0=v_banks[j][:].rearrange("p (h d) -> p h d", d=HEAD),
+                in1=ratios[j // TILES][:, s, :].unsqueeze(2).to_broadcast([P, GROUP_HEADS, HEAD]),
                 op=ALU.mult,
             )
             first = half * BANK + s * P
@@ -257,14 +316,27 @@ def tile_gatedlinearattention_pa_kernel(tc, hidden_states, Wq, Wk, Wv, out):
                 out=out_dram[first : first + P, group * BANK : (group + 1) * BANK], in_=z[:]
             )
 
-        finished = None
-        for group in range(GROUPS):
-            for half in range(HALVES):
-                sums = psum.tile([P, TILES, 2, GROUP_HEADS], F32, tag="sums")
-                for t in range(TILES):
-                    feature_round(group, half, t, sums)
-                    if finished is not None:
-                        value_tile(finished[0], finished[1], t, finished[2])
-                finished = (group, half, form_ratio(sums))
-        for s in range(TILES):
-            value_tile(finished[0], finished[1], s, finished[2])
+        turn_x(0)
+        regroup_w("q", 0)
+        quantise_x(0)
+        quantise_w("q", 0)
+        prepare("k", 0)
+        for r in range(AHEAD):
+            project(r, "q", a_banks, "a")
+            project(r, "k", c_banks, "c")
+        for r in range(ROUNDS + 1):
+            if r < ROUNDS:
+                feature_map(r)
+            scale_and_store(r - TILES - 1)
+            if r < ROUNDS:
+                form_products(r)
+            if 1 <= r <= len(later_operands):
+                prepare(later_operands[r - 1][0], later_operands[r - 1][1])
+            project(r + AHEAD, "q", a_banks, "a")
+            project(r + AHEAD, "k", c_banks, "c")
+            project_value(r - TILES)
+            if r >= TILES and r % TILES == 0:
+                head_sums(r // TILES - 1)
+        for j in range(ROUNDS - TILES, ROUNDS):
+            project_value(j + 1)
+            scale_and_store(j)

@@ -28,6 +28,7 @@ GROUP_HEADS = BANK // HEAD
 HEAD_ROWS = P // GROUP_HEADS
 ROUNDS = GROUPS * HALVES * TILES
 AHEAD = 2
+SUMS_LAG = 2
 NORM_EPS = 1e-6
 
 FLOPS = 3 * 2 * TOKENS * HIDDEN * HIDDEN
@@ -46,6 +47,7 @@ def tile_gatedlinearattention_pa_kernel(tc, hidden_states, Wq, Wk, Wv, out):
         work = pools.enter_context(tc.tile_pool(name="work", bufs=3))
         small = pools.enter_context(tc.tile_pool(name="small", bufs=4))
         products = pools.enter_context(tc.tile_pool(name="products", bufs=2 * TILES))
+        outgoing = pools.enter_context(tc.tile_pool(name="outgoing", bufs=5))
         psum = pools.enter_context(tc.psum_pool(name="psum", bufs=2))
         pools.enter_context(tc.manual_schedule())
 
@@ -131,7 +133,8 @@ def tile_gatedlinearattention_pa_kernel(tc, hidden_states, Wq, Wk, Wv, out):
 
         def regroup_w(w, group):
             order = "p (c i) t -> p c t i" if w == "v" else "p (i c) t -> p c t i"
-            for g, engine_copy in ((0, nc.scalar.copy), (1, nc.vector.tensor_copy)):
+            copy_of_pass_0 = nc.vector.tensor_copy if w == "v" else nc.scalar.copy
+            for g, engine_copy in ((0, copy_of_pass_0), (1, nc.vector.tensor_copy)):
                 grouped = stage.tile([P, BANK, PACK], BF16, tag="w_grouped", name="w_grouped_%s_%d_%d" % (w, group, g), align_bytes=64)
                 engine_copy(
                     out=grouped[:].rearrange(order, i=4),
@@ -224,8 +227,6 @@ def tile_gatedlinearattention_pa_kernel(tc, hidden_states, Wq, Wk, Wv, out):
         qs_tiles = {}
 
         def form_products(r):
-            qk = products.tile([P, BANK], F32)
-            nc.vector.tensor_tensor(out=qk[:], in0=q_tiles[r][:], in1=k_tiles[r][:], op=ALU.mult)
             qs = products.tile([P, BANK], F32)
             for b in range(BATCHES):
                 cols = slice(b * SEQ, (b + 1) * SEQ)
@@ -237,13 +238,15 @@ def tile_gatedlinearattention_pa_kernel(tc, hidden_states, Wq, Wk, Wv, out):
                     op0=ALU.mult,
                     op1=ALU.add,
                 )
+            qk = products.tile([P, BANK], F32)
+            nc.gpsimd.tensor_tensor(out=qk[:], in0=q_tiles[r][:], in1=k_tiles[r][:], op=ALU.mult)
             qk_tiles[r] = qk
             qs_tiles[r] = qs
 
         block_sums = {}
 
         def head_sums(block):
-            for kind, tiles in (("qk", qk_tiles), ("qs", qs_tiles)):
+            for kind, tiles in (("qs", qs_tiles), ("qk", qk_tiles)):
                 turned = psum.tile([P, TILES, P], F32, tag="sum_" + kind, name="sum_" + kind, bufs=1)
                 for s in range(TILES):
                     for t in range(TILES):
@@ -261,7 +264,7 @@ def tile_gatedlinearattention_pa_kernel(tc, hidden_states, Wq, Wk, Wv, out):
 
         def form_ratio(block):
             totals = {}
-            for kind in ("qk", "qs"):
+            for kind in ("qs", "qk"):
                 totals[kind] = small.tile([P, TILES * GROUP_HEADS], F32, name="total_" + kind)
                 nc.vector.tensor_reduce(
                     out=totals[kind][:],
@@ -304,7 +307,7 @@ def tile_gatedlinearattention_pa_kernel(tc, hidden_states, Wq, Wk, Wv, out):
             group, half, s = place(j)
             if s == 0:
                 form_ratio(j // TILES)
-            z = work.tile([P, BANK], F32)
+            z = outgoing.tile([P, BANK], F32)
             nc.vector.tensor_tensor(
                 out=z[:].rearrange("p (h d) -> p h d", d=HEAD),
                 in0=v_banks[j][:].rearrange("p (h d) -> p h d", d=HEAD),
@@ -316,27 +319,24 @@ def tile_gatedlinearattention_pa_kernel(tc, hidden_states, Wq, Wk, Wv, out):
                 out=out_dram[first : first + P, group * BANK : (group + 1) * BANK], in_=z[:]
             )
 
-        turn_x(0)
-        regroup_w("q", 0)
-        quantise_x(0)
-        quantise_w("q", 0)
+        prepare("x", 0)
+        prepare("q", 0)
         prepare("k", 0)
         for r in range(AHEAD):
             project(r, "q", a_banks, "a")
             project(r, "k", c_banks, "c")
-        for r in range(ROUNDS + 1):
+        for r in range(ROUNDS + SUMS_LAG + 1):
             if r < ROUNDS:
                 feature_map(r)
-            scale_and_store(r - TILES - 1)
-            if r < ROUNDS:
                 form_products(r)
+            scale_and_store(r - TILES - SUMS_LAG)
             if 1 <= r <= len(later_operands):
                 prepare(later_operands[r - 1][0], later_operands[r - 1][1])
+            if r >= TILES + SUMS_LAG - 1 and (r - SUMS_LAG + 1) % TILES == 0:
+                head_sums((r - SUMS_LAG + 1) // TILES - 1)
             project(r + AHEAD, "q", a_banks, "a")
             project(r + AHEAD, "k", c_banks, "c")
-            project_value(r - TILES)
-            if r >= TILES and r % TILES == 0:
-                head_sums(r // TILES - 1)
-        for j in range(ROUNDS - TILES, ROUNDS):
+            project_value(r - TILES - SUMS_LAG + 1)
+        for j in range(ROUNDS - TILES + 1, ROUNDS):
             project_value(j + 1)
             scale_and_store(j)

@@ -133,8 +133,7 @@ def tile_gatedlinearattention_pa_kernel(tc, hidden_states, Wq, Wk, Wv, out):
 
         def regroup_w(w, group):
             order = "p (c i) t -> p c t i" if w == "v" else "p (i c) t -> p c t i"
-            copy_of_pass_0 = nc.vector.tensor_copy if w == "v" else nc.scalar.copy
-            for g, engine_copy in ((0, copy_of_pass_0), (1, nc.vector.tensor_copy)):
+            for g, engine_copy in ((0, nc.scalar.copy), (1, nc.vector.tensor_copy)):
                 grouped = stage.tile([P, BANK, PACK], BF16, tag="w_grouped", name="w_grouped_%s_%d_%d" % (w, group, g), align_bytes=64)
                 engine_copy(
                     out=grouped[:].rearrange(order, i=4),
@@ -194,28 +193,28 @@ def tile_gatedlinearattention_pa_kernel(tc, hidden_states, Wq, Wk, Wv, out):
         def feature_map(r):
             a = a_banks[r]
             c = c_banks[r]
-            exp_a = work.tile([P, BANK], F32)
-            relu_a = work.tile([P, BANK], F32)
-            exp_c = work.tile([P, BANK], F32)
-            relu_c = work.tile([P, BANK], F32)
-            nc.scalar.activation(out=exp_a[:], in_=a[:], func=ACT.Exp)
-            nc.scalar.activation(out=relu_a[:], in_=a[:], func=ACT.Relu)
-            nc.scalar.activation(out=exp_c[:], in_=c[:], func=ACT.Exp)
-            nc.scalar.activation(out=relu_c[:], in_=c[:], func=ACT.Relu)
+            minus_a = work.tile([P, BANK], F32)
+            minus_c = work.tile([P, BANK], F32)
+            small_a = work.tile([P, BANK], F32)
+            small_c = work.tile([P, BANK], F32)
+            nc.scalar.activation(out=minus_a[:], in_=a[:], func=ACT.Relu, scale=-1.0)
+            nc.scalar.activation(out=minus_c[:], in_=c[:], func=ACT.Relu, scale=-1.0)
+            nc.scalar.activation(out=small_a[:], in_=minus_a[:], func=ACT.Exp, scale=-1.0)
+            nc.scalar.activation(out=small_c[:], in_=minus_c[:], func=ACT.Exp, scale=-1.0)
             q = work.tile([P, BANK], F32)
             k = work.tile([P, BANK], F32)
             k_sum = small.tile([P, BATCHES], F32)
             nc.vector.scalar_tensor_tensor(
-                out=q[:], in0=exp_a[:], scalar=1.0, in1=relu_a[:], op0=ALU.min, op1=ALU.add
+                out=q[:], in0=a[:], scalar=0.0, in1=small_a[:], op0=ALU.max, op1=ALU.add
             )
             for b in range(BATCHES):
                 cols = slice(b * SEQ, (b + 1) * SEQ)
                 nc.vector.scalar_tensor_tensor(
                     out=k[:, cols],
-                    in0=exp_c[:, cols],
-                    scalar=1.0,
-                    in1=relu_c[:, cols],
-                    op0=ALU.min,
+                    in0=c[:, cols],
+                    scalar=0.0,
+                    in1=small_c[:, cols],
+                    op0=ALU.max,
                     op1=ALU.add,
                     accum_out=k_sum[:, b : b + 1],
                 )

@@ -49,7 +49,6 @@ def tile_gatedlinearattention_pa_kernel(tc, hidden_states, Wq, Wk, Wv, out):
         products = pools.enter_context(tc.tile_pool(name="products", bufs=2 * TILES))
         outgoing = pools.enter_context(tc.tile_pool(name="outgoing", bufs=5))
         psum = pools.enter_context(tc.psum_pool(name="psum", bufs=2))
-        pools.enter_context(tc.manual_schedule())
 
         identity = const.tile([P, P], F32)
         make_identity(nc, identity[:])

@@ -237,7 +237,7 @@ def tile_gatedlinearattention_pa_kernel(tc, hidden_states, Wq, Wk, Wv, out):
                     op1=ALU.add,
                 )
             qk = products.tile([P, BANK], F32)
-            nc.gpsimd.tensor_tensor(out=qk[:], in0=q_tiles[r][:], in1=k_tiles[r][:], op=ALU.mult)
+            nc.vector.tensor_tensor(out=qk[:], in0=q_tiles[r][:], in1=k_tiles[r][:], op=ALU.mult)
             qk_tiles[r] = qk
             qs_tiles[r] = qs
 

@@ -228,14 +228,19 @@ def tile_gatedlinearattention_pa_kernel(tc, hidden_states, Wq, Wk, Wv, out):
             qs = products.tile([P, BANK], F32)
             for b in range(BATCHES):
                 cols = slice(b * SEQ, (b + 1) * SEQ)
-                nc.gpsimd.tensor_scalar(
-                    out=qs[:, cols],
-                    in0=q_tiles[r][:, cols],
-                    scalar1=k_sums[r][:, b : b + 1],
-                    scalar2=0.0,
-                    op0=ALU.mult,
-                    op1=ALU.add,
-                )
+                if r <= len(later_operands):
+                    nc.vector.tensor_scalar(
+                        out=qs[:, cols],
+                        in0=q_tiles[r][:, cols],
+                        scalar1=k_sums[r][:, b : b + 1],
+                        scalar2=0.0,
+                        op0=ALU.mult,
+                        op1=ALU.add,
+                    )
+                else:
+                    nc.scalar.activation(
+                        out=qs[:, cols], in_=q_tiles[r][:, cols], func=ACT.Copy, scale=k_sums[r][:, b : b + 1]
+                    )
             qk = products.tile([P, BANK], F32)
             nc.vector.tensor_tensor(out=qk[:], in0=q_tiles[r][:], in1=k_tiles[r][:], op=ALU.mult)
             qk_tiles[r] = qk

@@ -43,7 +43,7 @@ def tile_gatedlinearattention_pa_kernel(tc, hidden_states, Wq, Wk, Wv, out):
     with ExitStack() as pools:
         const = pools.enter_context(tc.tile_pool(name="const", bufs=1))
         keep = pools.enter_context(tc.tile_pool(name="keep", bufs=1))
-        stage = pools.enter_context(tc.tile_pool(name="stage", bufs=4))
+        stage = pools.enter_context(tc.tile_pool(name="stage", bufs=2))
         work = pools.enter_context(tc.tile_pool(name="work", bufs=3))
         small = pools.enter_context(tc.tile_pool(name="small", bufs=4))
         products = pools.enter_context(tc.tile_pool(name="products", bufs=2 * TILES))
@@ -117,12 +117,11 @@ def tile_gatedlinearattention_pa_kernel(tc, hidden_states, Wq, Wk, Wv, out):
         def quantise_x(half):
             codes = keep.tile([P, PASSES, BANK], U32, name="x_codes_%d" % half, align_bytes=64)
             scales = keep.tile([P, PASSES, BANK], U8, name="x_scales_%d" % half, align_bytes=64)
-            for g in range(PASSES):
-                nc.vector.quantize_mx(
-                    out=codes[:, g, :].bitcast(FP8X4),
-                    scales=scales[:, g, :],
-                    in_=x_grouped[half][:, g * BANK * PACK : (g + 1) * BANK * PACK],
-                )
+            nc.vector.quantize_mx(
+                out=codes[:].rearrange("p g n -> p (g n)").bitcast(FP8X4),
+                scales=scales[:].rearrange("p g n -> p (g n)"),
+                in_=x_grouped[half][:],
+            )
             x_codes[half] = codes
             x_scales[half] = scales
 
@@ -132,23 +131,22 @@ def tile_gatedlinearattention_pa_kernel(tc, hidden_states, Wq, Wk, Wv, out):
 
         def regroup_w(w, group):
             order = "p (c i) t -> p c t i" if w == "v" else "p (i c) t -> p c t i"
+            grouped = stage.tile([P, PASSES, BANK, PACK], BF16, tag="w_grouped", name="w_grouped_%s_%d" % (w, group), align_bytes=64)
             for g, engine_copy in ((0, nc.scalar.copy), (1, nc.vector.tensor_copy)):
-                grouped = stage.tile([P, BANK, PACK], BF16, tag="w_grouped", name="w_grouped_%s_%d_%d" % (w, group, g), align_bytes=64)
                 engine_copy(
-                    out=grouped[:].rearrange(order, i=4),
+                    out=grouped[:, g, :, :].rearrange(order, i=4),
                     in_=w_raw[(w, group, g)][:].rearrange("p t (c i) -> p c t i", i=4),
                 )
-                w_grouped[(w, group, g)] = grouped
+            w_grouped[(w, group)] = grouped
 
         def quantise_w(w, group):
             codes = keep.tile([P, PASSES, BANK], U32, name="w_codes_%s_%d" % (w, group), align_bytes=64)
             scales = keep.tile([P, PASSES, BANK], U8, name="w_scales_%s_%d" % (w, group), align_bytes=64)
-            for g in range(PASSES):
-                nc.vector.quantize_mx(
-                    out=codes[:, g, :].bitcast(FP8X4),
-                    scales=scales[:, g, :],
-                    in_=w_grouped[(w, group, g)][:].rearrange("p n t -> p (n t)"),
-                )
+            nc.vector.quantize_mx(
+                out=codes[:].rearrange("p g n -> p (g n)").bitcast(FP8X4),
+                scales=scales[:].rearrange("p g n -> p (g n)"),
+                in_=w_grouped[(w, group)][:].rearrange("p g n t -> p (g n t)"),
+            )
             w_codes[(w, group)] = codes
             w_scales[(w, group)] = scales
 

@@ -29,6 +29,7 @@ HEAD_ROWS = P // GROUP_HEADS
 ROUNDS = GROUPS * HALVES * TILES
 AHEAD = 2
 SUMS_LAG = 2
+LAST_BLOCK = ROUNDS // TILES - 1
 NORM_EPS = 1e-6
 
 FLOPS = 3 * 2 * TOKENS * HIDDEN * HIDDEN
@@ -231,13 +232,17 @@ def tile_gatedlinearattention_pa_kernel(tc, hidden_states, Wq, Wk, Wv, out):
                         out=qs[:, cols],
                         in0=q_tiles[r][:, cols],
                         scalar1=k_sums[r][:, b : b + 1],
-                        scalar2=0.0,
+                        scalar2=NORM_EPS / HEAD,
                         op0=ALU.mult,
                         op1=ALU.add,
                     )
                 else:
                     nc.scalar.activation(
-                        out=qs[:, cols], in_=q_tiles[r][:, cols], func=ACT.Copy, scale=k_sums[r][:, b : b + 1]
+                        out=qs[:, cols],
+                        in_=q_tiles[r][:, cols],
+                        func=ACT.Copy,
+                        scale=k_sums[r][:, b : b + 1],
+                        bias=NORM_EPS / HEAD,
                     )
             qk = products.tile([P, BANK], F32)
             nc.vector.tensor_tensor(out=qk[:], in0=q_tiles[r][:], in1=k_tiles[r][:], op=ALU.mult)
@@ -246,38 +251,51 @@ def tile_gatedlinearattention_pa_kernel(tc, hidden_states, Wq, Wk, Wv, out):
 
         block_sums = {}
 
-        def head_sums(block):
-            for kind, tiles in (("qs", qs_tiles), ("qk", qk_tiles)):
-                turned = psum.tile([P, TILES, P], F32, tag="sum_" + kind, name="sum_" + kind, bufs=1)
+        def head_sums(block, first=0, last=TILES, late=False):
+            for kind, tiles, late_tag in (("qs", qs_tiles, "a"), ("qk", qk_tiles, "c")):
+                if late:
+                    turned = psum.tile([P, TILES, P], F32, tag=late_tag, name=late_tag)
+                else:
+                    turned = psum.tile([P, TILES, P], F32, tag="sum_" + kind, name="sum_" + kind, bufs=1)
                 for s in range(TILES):
-                    for t in range(TILES):
+                    for t in range(first, last):
                         nc.tensor.matmul(
                             out=turned[:, s, :],
                             lhsT=tiles[block * TILES + t][:, s * P : (s + 1) * P],
                             rhs=identity[:],
                             is_transpose=True,
-                            start=(t == 0),
-                            stop=(t == TILES - 1),
+                            start=(t == first),
+                            stop=(t == last - 1),
                         )
-                block_sums[(kind, block)] = turned
+                block_sums[(kind, block, late)] = turned
 
         ratios = {}
 
+        early_totals = {}
+
+        def reduce_sums(kind, block, late):
+            total = small.tile([P, TILES * GROUP_HEADS], F32, name="total_%s_%d" % (kind, late))
+            nc.vector.tensor_reduce(
+                out=total[:],
+                in_=block_sums[(kind, block, late)][:].rearrange("p s (h e) -> p (s h) e", e=HEAD_ROWS),
+                axis=mybir.AxisListType.X,
+                op=ALU.add,
+            )
+            return total
+
         def form_ratio(block):
+            split = block == LAST_BLOCK
             totals = {}
             for kind in ("qs", "qk"):
-                totals[kind] = small.tile([P, TILES * GROUP_HEADS], F32, name="total_" + kind)
-                nc.vector.tensor_reduce(
-                    out=totals[kind][:],
-                    in_=block_sums[(kind, block)][:].rearrange("p s (h e) -> p (s h) e", e=HEAD_ROWS),
-                    axis=mybir.AxisListType.X,
-                    op=ALU.add,
-                )
-            normalizer = small.tile([P, TILES * GROUP_HEADS], F32)
+                totals[kind] = reduce_sums(kind, block, split)
             inverse = small.tile([P, TILES * GROUP_HEADS], F32)
             ratio = small.tile([P, TILES, GROUP_HEADS], F32)
-            nc.vector.tensor_scalar_add(out=normalizer[:], in0=totals["qs"][:], scalar1=NORM_EPS)
-            nc.vector.reciprocal(out=inverse[:], in_=normalizer[:])
+            if split:
+                for kind in ("qs", "qk"):
+                    whole = small.tile([P, TILES * GROUP_HEADS], F32, name="whole_" + kind)
+                    nc.vector.tensor_tensor(out=whole[:], in0=totals[kind][:], in1=early_totals[kind][:], op=ALU.add)
+                    totals[kind] = whole
+            nc.vector.reciprocal(out=inverse[:], in_=totals["qs"][:])
             nc.vector.tensor_tensor(
                 out=ratio[:].rearrange("p s h -> p (s h)"), in0=totals["qk"][:], in1=inverse[:], op=ALU.mult
             )
@@ -285,11 +303,15 @@ def tile_gatedlinearattention_pa_kernel(tc, hidden_states, Wq, Wk, Wv, out):
 
         v_banks = {}
 
+        def by_scalar(j):
+            return j + TILES + SUMS_LAG >= ROUNDS and (j < ROUNDS - TILES or j % 2 == 1)
+
         def project_value(j):
             if not 0 <= j < ROUNDS:
                 return
             group, half, s = place(j)
-            v = psum.tile([P, BANK], F32, tag="v")
+            tag = ("a" if j in (ROUNDS - 6, ROUNDS - 3) else "c") if by_scalar(j) else "v"
+            v = psum.tile([P, BANK], F32, tag=tag, name=tag)
             for g in range(PASSES):
                 nc.tensor.matmul_mx(
                     out=v[:],
@@ -309,12 +331,19 @@ def tile_gatedlinearattention_pa_kernel(tc, hidden_states, Wq, Wk, Wv, out):
             if s == 0:
                 form_ratio(j // TILES)
             z = outgoing.tile([P, BANK], F32)
-            nc.vector.tensor_tensor(
-                out=z[:].rearrange("p (h d) -> p h d", d=HEAD),
-                in0=v_banks[j][:].rearrange("p (h d) -> p h d", d=HEAD),
-                in1=ratios[j // TILES][:, s, :].unsqueeze(2).to_broadcast([P, GROUP_HEADS, HEAD]),
-                op=ALU.mult,
-            )
+            if by_scalar(j):
+                for h in range(GROUP_HEADS):
+                    cols = slice(h * HEAD, (h + 1) * HEAD)
+                    nc.scalar.activation(
+                        out=z[:, cols], in_=v_banks[j][:, cols], func=ACT.Copy, scale=ratios[j // TILES][:, s, h : h + 1]
+                    )
+            else:
+                nc.vector.tensor_tensor(
+                    out=z[:].rearrange("p (h d) -> p h d", d=HEAD),
+                    in0=v_banks[j][:].rearrange("p (h d) -> p h d", d=HEAD),
+                    in1=ratios[j // TILES][:, s, :].unsqueeze(2).to_broadcast([P, GROUP_HEADS, HEAD]),
+                    op=ALU.mult,
+                )
             first = half * BANK + s * P
             nc.sync.dma_start(
                 out=out_dram[first : first + P, group * BANK : (group + 1) * BANK], in_=z[:]
@@ -333,8 +362,17 @@ def tile_gatedlinearattention_pa_kernel(tc, hidden_states, Wq, Wk, Wv, out):
             scale_and_store(r - TILES - SUMS_LAG)
             if 1 <= r <= len(later_operands):
                 prepare(later_operands[r - 1][0], later_operands[r - 1][1])
+            if r == ROUNDS:
+                for kind in ("qs", "qk"):
+                    early_totals[kind] = reduce_sums(kind, LAST_BLOCK, False)
+            if r == ROUNDS - 1:
+                head_sums(LAST_BLOCK, 0, TILES - 1)
             if r >= TILES + SUMS_LAG - 1 and (r - SUMS_LAG + 1) % TILES == 0:
-                head_sums((r - SUMS_LAG + 1) // TILES - 1)
+                block = (r - SUMS_LAG + 1) // TILES - 1
+                if block == LAST_BLOCK:
+                    head_sums(block, TILES - 1, TILES, late=True)
+                else:
+                    head_sums(block)
             project(r + AHEAD, "q", a_banks, "a")
             project(r + AHEAD, "k", c_banks, "c")
             project_value(r - TILES - SUMS_LAG + 1)

@@ -30,6 +30,7 @@ ROUNDS = GROUPS * HALVES * TILES
 AHEAD = 2
 SUMS_LAG = 2
 LAST_BLOCK = ROUNDS // TILES - 1
+COLUMN_TILES = 4
 NORM_EPS = 1e-6
 
 FLOPS = 3 * 2 * TOKENS * HIDDEN * HIDDEN
@@ -53,6 +54,19 @@ def tile_gatedlinearattention_pa_kernel(tc, hidden_states, Wq, Wk, Wv, out):
 
         identity = const.tile([P, P], F32)
         make_identity(nc, identity[:])
+        head_mask = const.tile([P, BATCHES, GROUP_HEADS], F32)
+        for b in range(BATCHES):
+            nc.vector.tensor_reduce(
+                out=head_mask[:, b, :],
+                in_=identity[:].rearrange("p (h e) -> p h e", e=HEAD_ROWS),
+                axis=mybir.AxisListType.X,
+                op=ALU.add,
+            )
+        k_sum_columns = []
+        for i in range(COLUMN_TILES):
+            columns = const.tile([P, P], F32, name="k_sum_columns_%d" % i)
+            nc.vector.memset(columns[:], 0.0)
+            k_sum_columns.append(columns)
         warm = const.tile([P, 2], F32)
         nc.vector.memset(warm[:], 0.0)
         nc.scalar.activation(out=warm[:, 1:2], in_=warm[:, 0:1], func=ACT.Exp)
@@ -216,43 +230,60 @@ def tile_gatedlinearattention_pa_kernel(tc, hidden_states, Wq, Wk, Wv, out):
                     op1=ALU.add,
                     accum_out=k_sum[:, b : b + 1],
                 )
+            nc.vector.tensor_tensor(
+                out=k_sum_columns[r % COLUMN_TILES][:, 0 : BATCHES * GROUP_HEADS].rearrange("p (b h) -> p b h", b=BATCHES),
+                in0=head_mask[:],
+                in1=k_sum[:].unsqueeze(2).to_broadcast([P, BATCHES, GROUP_HEADS]),
+                op=ALU.mult,
+            )
             q_tiles[r] = q
             k_tiles[r] = k
             k_sums[r] = k_sum
 
         qk_tiles = {}
-        qs_tiles = {}
 
         def form_products(r):
-            qs = products.tile([P, BANK], F32)
-            for b in range(BATCHES):
-                cols = slice(b * SEQ, (b + 1) * SEQ)
-                if r <= len(later_operands):
-                    nc.vector.tensor_scalar(
-                        out=qs[:, cols],
-                        in0=q_tiles[r][:, cols],
-                        scalar1=k_sums[r][:, b : b + 1],
-                        scalar2=NORM_EPS / HEAD,
-                        op0=ALU.mult,
-                        op1=ALU.add,
-                    )
-                else:
-                    nc.scalar.activation(
-                        out=qs[:, cols],
-                        in_=q_tiles[r][:, cols],
-                        func=ACT.Copy,
-                        scale=k_sums[r][:, b : b + 1],
-                        bias=NORM_EPS / HEAD,
-                    )
             qk = products.tile([P, BANK], F32)
             nc.vector.tensor_tensor(out=qk[:], in0=q_tiles[r][:], in1=k_tiles[r][:], op=ALU.mult)
             qk_tiles[r] = qk
-            qs_tiles[r] = qs
+
+        norm_banks = {}
+        inverses = {}
+
+        def add_normalizer(r):
+            if r >= ROUNDS:
+                return
+            block, t = divmod(r, TILES)
+            if t == 0:
+                norm_banks[block] = psum.tile([P, BANK], F32, tag="norm", name="norm", bufs=1)
+            nc.tensor.matmul(
+                out=norm_banks[block][:],
+                lhsT=k_sum_columns[r % COLUMN_TILES][:],
+                rhs=q_tiles[r][:],
+                start=(t == 0),
+                stop=(t == TILES - 1),
+            )
+
+        def turn_normalizer(block):
+            rows = work.tile([P, BANK], F32, name="norm_rows")
+            nc.scalar.activation(out=rows[:], in_=norm_banks[block][:], func=ACT.Copy, bias=NORM_EPS)
+            tag = "a" if block == LAST_BLOCK else "v"
+            turned = psum.tile([P, TILES, P], F32, tag=tag, name=tag)
+            for s in range(TILES):
+                nc.tensor.transpose(out=turned[:, s, :], in_=rows[:, s * P : (s + 1) * P], identity=identity[:])
+            inverse = small.tile([P, TILES, GROUP_HEADS], F32)
+            per_batch = TILES // BATCHES
+            for b in range(BATCHES):
+                nc.vector.reciprocal(
+                    out=inverse[:, b * per_batch : (b + 1) * per_batch, :],
+                    in_=turned[:, b * per_batch : (b + 1) * per_batch, b * GROUP_HEADS : (b + 1) * GROUP_HEADS],
+                )
+            inverses[block] = inverse
 
         block_sums = {}
 
         def head_sums(block, first=0, last=TILES, late=False):
-            for kind, tiles, late_tag in (("qs", qs_tiles, "a"), ("qk", qk_tiles, "c")):
+            for kind, tiles, late_tag in (("qk", qk_tiles, "c"),):
                 if late:
                     turned = psum.tile([P, TILES, P], F32, tag=late_tag, name=late_tag)
                 else:
@@ -285,19 +316,17 @@ def tile_gatedlinearattention_pa_kernel(tc, hidden_states, Wq, Wk, Wv, out):
 
         def form_ratio(block):
             split = block == LAST_BLOCK
-            totals = {}
-            for kind in ("qs", "qk"):
-                totals[kind] = reduce_sums(kind, block, split)
-            inverse = small.tile([P, TILES * GROUP_HEADS], F32)
+            total = reduce_sums("qk", block, split)
             ratio = small.tile([P, TILES, GROUP_HEADS], F32)
             if split:
-                for kind in ("qs", "qk"):
-                    whole = small.tile([P, TILES * GROUP_HEADS], F32, name="whole_" + kind)
-                    nc.vector.tensor_tensor(out=whole[:], in0=totals[kind][:], in1=early_totals[kind][:], op=ALU.add)
-                    totals[kind] = whole
-            nc.vector.reciprocal(out=inverse[:], in_=totals["qs"][:])
+                whole = small.tile([P, TILES * GROUP_HEADS], F32, name="whole_qk")
+                nc.vector.tensor_tensor(out=whole[:], in0=total[:], in1=early_totals["qk"][:], op=ALU.add)
+                total = whole
             nc.vector.tensor_tensor(
-                out=ratio[:].rearrange("p s h -> p (s h)"), in0=totals["qk"][:], in1=inverse[:], op=ALU.mult
+                out=ratio[:].rearrange("p s h -> p (s h)"),
+                in0=total[:],
+                in1=inverses[block][:].rearrange("p s h -> p (s h)"),
+                op=ALU.mult,
             )
             ratios[block] = ratio
 
@@ -360,11 +389,12 @@ def tile_gatedlinearattention_pa_kernel(tc, hidden_states, Wq, Wk, Wv, out):
                 feature_map(r)
                 form_products(r)
             scale_and_store(r - TILES - SUMS_LAG)
+            if r >= TILES and r % TILES == 0:
+                turn_normalizer(r // TILES - 1)
             if 1 <= r <= len(later_operands):
                 prepare(later_operands[r - 1][0], later_operands[r - 1][1])
             if r == ROUNDS:
-                for kind in ("qs", "qk"):
-                    early_totals[kind] = reduce_sums(kind, LAST_BLOCK, False)
+                early_totals["qk"] = reduce_sums("qk", LAST_BLOCK, False)
             if r == ROUNDS - 1:
                 head_sums(LAST_BLOCK, 0, TILES - 1)
             if r >= TILES + SUMS_LAG - 1 and (r - SUMS_LAG + 1) % TILES == 0:
@@ -376,6 +406,7 @@ def tile_gatedlinearattention_pa_kernel(tc, hidden_states, Wq, Wk, Wv, out):
             project(r + AHEAD, "q", a_banks, "a")
             project(r + AHEAD, "k", c_banks, "c")
             project_value(r - TILES - SUMS_LAG + 1)
+            add_normalizer(r)
         for j in range(ROUNDS - TILES + 1, ROUNDS):
             project_value(j + 1)
             scale_and_store(j)

@@ -31,6 +31,7 @@ AHEAD = 2
 SUMS_LAG = 2
 LAST_BLOCK = ROUNDS // TILES - 1
 COLUMN_TILES = 4
+MATMUL_BLOCKS = 2
 NORM_EPS = 1e-6
 
 FLOPS = 3 * 2 * TOKENS * HIDDEN * HIDDEN
@@ -123,7 +124,7 @@ def tile_gatedlinearattention_pa_kernel(tc, hidden_states, Wq, Wk, Wv, out):
                         nc.tensor.transpose(
                             out=turned[:, g, u, :], in_=words[:, g, u, :], identity=identity[:]
                         )
-                nc.scalar.copy(
+                (nc.scalar.copy if half == 0 else nc.vector.tensor_copy)(
                     out=grouped_words[:, :, i * P : (i + 1) * P, :],
                     in_=turned[:].rearrange("p g u r -> p g r u"),
                 )
@@ -230,19 +231,33 @@ def tile_gatedlinearattention_pa_kernel(tc, hidden_states, Wq, Wk, Wv, out):
                     op1=ALU.add,
                     accum_out=k_sum[:, b : b + 1],
                 )
-            nc.vector.tensor_tensor(
-                out=k_sum_columns[r % COLUMN_TILES][:, 0 : BATCHES * GROUP_HEADS].rearrange("p (b h) -> p b h", b=BATCHES),
-                in0=head_mask[:],
-                in1=k_sum[:].unsqueeze(2).to_broadcast([P, BATCHES, GROUP_HEADS]),
-                op=ALU.mult,
-            )
+            if r // TILES < MATMUL_BLOCKS:
+                nc.vector.tensor_tensor(
+                    out=k_sum_columns[r % COLUMN_TILES][:, 0 : BATCHES * GROUP_HEADS].rearrange("p (b h) -> p b h", b=BATCHES),
+                    in0=head_mask[:],
+                    in1=k_sum[:].unsqueeze(2).to_broadcast([P, BATCHES, GROUP_HEADS]),
+                    op=ALU.mult,
+                )
             q_tiles[r] = q
             k_tiles[r] = k
             k_sums[r] = k_sum
 
         qk_tiles = {}
+        qs_tiles = {}
 
         def form_products(r):
+            if r // TILES >= MATMUL_BLOCKS:
+                qs = products.tile([P, BANK], F32)
+                for b in range(BATCHES):
+                    cols = slice(b * SEQ, (b + 1) * SEQ)
+                    nc.scalar.activation(
+                        out=qs[:, cols],
+                        in_=q_tiles[r][:, cols],
+                        func=ACT.Copy,
+                        scale=k_sums[r][:, b : b + 1],
+                        bias=NORM_EPS / HEAD,
+                    )
+                qs_tiles[r] = qs
             qk = products.tile([P, BANK], F32)
             nc.vector.tensor_tensor(out=qk[:], in0=q_tiles[r][:], in1=k_tiles[r][:], op=ALU.mult)
             qk_tiles[r] = qk
@@ -251,11 +266,11 @@ def tile_gatedlinearattention_pa_kernel(tc, hidden_states, Wq, Wk, Wv, out):
         inverses = {}
 
         def add_normalizer(r):
-            if r >= ROUNDS:
+            if r >= MATMUL_BLOCKS * TILES:
                 return
             block, t = divmod(r, TILES)
             if t == 0:
-                norm_banks[block] = psum.tile([P, BANK], F32, tag="norm", name="norm", bufs=1)
+                norm_banks[block] = psum.tile([P, BANK], F32, tag="sum_qs", name="sum_qs", bufs=1)
             nc.tensor.matmul(
                 out=norm_banks[block][:],
                 lhsT=k_sum_columns[r % COLUMN_TILES][:],
@@ -267,8 +282,7 @@ def tile_gatedlinearattention_pa_kernel(tc, hidden_states, Wq, Wk, Wv, out):
         def turn_normalizer(block):
             rows = work.tile([P, BANK], F32, name="norm_rows")
             nc.scalar.activation(out=rows[:], in_=norm_banks[block][:], func=ACT.Copy, bias=NORM_EPS)
-            tag = "a" if block == LAST_BLOCK else "v"
-            turned = psum.tile([P, TILES, P], F32, tag=tag, name=tag)
+            turned = psum.tile([P, TILES, P], F32, tag="v", name="v")
             for s in range(TILES):
                 nc.tensor.transpose(out=turned[:, s, :], in_=rows[:, s * P : (s + 1) * P], identity=identity[:])
             inverse = small.tile([P, TILES, GROUP_HEADS], F32)
@@ -283,7 +297,9 @@ def tile_gatedlinearattention_pa_kernel(tc, hidden_states, Wq, Wk, Wv, out):
         block_sums = {}
 
         def head_sums(block, first=0, last=TILES, late=False):
-            for kind, tiles, late_tag in (("qk", qk_tiles, "c"),):
+            for kind, tiles, late_tag in (("qs", qs_tiles, "a"), ("qk", qk_tiles, "c")):
+                if kind == "qs" and block < MATMUL_BLOCKS:
+                    continue
                 if late:
                     turned = psum.tile([P, TILES, P], F32, tag=late_tag, name=late_tag)
                 else:
@@ -316,15 +332,22 @@ def tile_gatedlinearattention_pa_kernel(tc, hidden_states, Wq, Wk, Wv, out):
 
         def form_ratio(block):
             split = block == LAST_BLOCK
-            total = reduce_sums("qk", block, split)
+            totals = {}
+            for kind in ("qs", "qk") if block >= MATMUL_BLOCKS else ("qk",):
+                totals[kind] = reduce_sums(kind, block, split)
             ratio = small.tile([P, TILES, GROUP_HEADS], F32)
             if split:
-                whole = small.tile([P, TILES * GROUP_HEADS], F32, name="whole_qk")
-                nc.vector.tensor_tensor(out=whole[:], in0=total[:], in1=early_totals["qk"][:], op=ALU.add)
-                total = whole
+                for kind in ("qs", "qk"):
+                    whole = small.tile([P, TILES * GROUP_HEADS], F32, name="whole_" + kind)
+                    nc.vector.tensor_tensor(out=whole[:], in0=totals[kind][:], in1=early_totals[kind][:], op=ALU.add)
+                    totals[kind] = whole
+            if block >= MATMUL_BLOCKS:
+                inverse = small.tile([P, TILES, GROUP_HEADS], F32)
+                nc.vector.reciprocal(out=inverse[:].rearrange("p s h -> p (s h)"), in_=totals["qs"][:])
+                inverses[block] = inverse
             nc.vector.tensor_tensor(
                 out=ratio[:].rearrange("p s h -> p (s h)"),
-                in0=total[:],
+                in0=totals["qk"][:],
                 in1=inverses[block][:].rearrange("p s h -> p (s h)"),
                 op=ALU.mult,
             )
@@ -389,12 +412,13 @@ def tile_gatedlinearattention_pa_kernel(tc, hidden_states, Wq, Wk, Wv, out):
                 feature_map(r)
                 form_products(r)
             scale_and_store(r - TILES - SUMS_LAG)
-            if r >= TILES and r % TILES == 0:
+            if r % TILES == 0 and 1 <= r // TILES <= MATMUL_BLOCKS:
                 turn_normalizer(r // TILES - 1)
             if 1 <= r <= len(later_operands):
                 prepare(later_operands[r - 1][0], later_operands[r - 1][1])
             if r == ROUNDS:
-                early_totals["qk"] = reduce_sums("qk", LAST_BLOCK, False)
+                for kind in ("qs", "qk"):
+                    early_totals[kind] = reduce_sums(kind, LAST_BLOCK, False)
             if r == ROUNDS - 1:
                 head_sums(LAST_BLOCK, 0, TILES - 1)
             if r >= TILES + SUMS_LAG - 1 and (r - SUMS_LAG + 1) % TILES == 0:

@@ -147,7 +147,8 @@ def tile_gatedlinearattention_pa_kernel(tc, hidden_states, Wq, Wk, Wv, out):
 
         def regroup_w(w, group):
             order = "p (c i) t -> p c t i" if w == "v" else "p (i c) t -> p c t i"
-            grouped = stage.tile([P, PASSES, BANK, PACK], BF16, tag="w_grouped", name="w_grouped_%s_%d" % (w, group), align_bytes=64)
+            tag = "w_grouped_first" if (w, group) == ("q", 0) else "w_grouped"
+            grouped = stage.tile([P, PASSES, BANK, PACK], BF16, tag=tag, name="w_grouped_%s_%d" % (w, group), bufs=1, align_bytes=64)
             for g, engine_copy in ((0, nc.scalar.copy), (1, nc.vector.tensor_copy)):
                 engine_copy(
                     out=grouped[:, g, :, :].rearrange(order, i=4),
@@ -401,12 +402,18 @@ def tile_gatedlinearattention_pa_kernel(tc, hidden_states, Wq, Wk, Wv, out):
                 out=out_dram[first : first + P, group * BANK : (group + 1) * BANK], in_=z[:]
             )
 
-        prepare("x", 0)
-        prepare("q", 0)
-        prepare("k", 0)
-        for r in range(AHEAD):
-            project(r, "q", a_banks, "a")
-            project(r, "k", c_banks, "c")
+        with tc.manual_schedule(engines={mybir.EngineType.PE, mybir.EngineType.Activation, mybir.EngineType.DVE}):
+            turn_x(0)
+            regroup_w("q", 0)
+            quantise_x(0)
+            regroup_w("k", 0)
+            quantise_w("q", 0)
+            for r in range(AHEAD):
+                project(r, "q", a_banks, "a")
+            quantise_w("k", 0)
+            for r in range(AHEAD):
+                project(r, "k", c_banks, "c")
+            prepare(later_operands[0][0], later_operands[0][1])
         for r in range(ROUNDS + SUMS_LAG + 1):
             if r < ROUNDS:
                 feature_map(r)
@@ -414,7 +421,7 @@ def tile_gatedlinearattention_pa_kernel(tc, hidden_states, Wq, Wk, Wv, out):
             scale_and_store(r - TILES - SUMS_LAG)
             if r % TILES == 0 and 1 <= r // TILES <= MATMUL_BLOCKS:
                 turn_normalizer(r // TILES - 1)
-            if 1 <= r <= len(later_operands):
+            if 2 <= r <= len(later_operands):
                 prepare(later_operands[r - 1][0], later_operands[r - 1][1])
             if r == ROUNDS:
                 for kind in ("qs", "qk"):

from contextlib import ExitStack

import concourse.mybir as mybir
from concourse.masks import make_identity

F32 = mybir.dt.float32
BF16 = mybir.dt.bfloat16
U32 = mybir.dt.uint32
U8 = mybir.dt.uint8
FP8X4 = mybir.dt.float8_e4m3fn_x4
ALU = mybir.AluOpType
ACT = mybir.ActivationFunctionType

P = 128
PACK = 4
K_PASS = P * PACK
TOKENS = 1024
SEQ = 256
HIDDEN = 1024
HEAD = 64
PASSES = HIDDEN // K_PASS
BANK = 512
HALVES = TOKENS // BANK
GROUPS = HIDDEN // BANK
TILES = BANK // P
BATCHES = BANK // SEQ
GROUP_HEADS = BANK // HEAD
HEAD_ROWS = P // GROUP_HEADS
ROUNDS = GROUPS * HALVES * TILES
AHEAD = 2
SUMS_LAG = 2
LAST_BLOCK = ROUNDS // TILES - 1
COLUMN_TILES = 4
MATMUL_BLOCKS = 2
NORM_EPS = 1e-6

FLOPS = 3 * 2 * TOKENS * HIDDEN * HIDDEN


def tile_gatedlinearattention_pa_kernel(tc, hidden_states, Wq, Wk, Wv, out):
    nc = tc.nc
    x_dram = hidden_states.flatten_outer_dims()
    out_dram = out.flatten_outer_dims()
    weight_dram = {"q": Wq, "k": Wk, "v": Wv}

    with ExitStack() as pools:
        const = pools.enter_context(tc.tile_pool(name="const", bufs=1))
        keep = pools.enter_context(tc.tile_pool(name="keep", bufs=1))
        stage = pools.enter_context(tc.tile_pool(name="stage", bufs=2))
        work = pools.enter_context(tc.tile_pool(name="work", bufs=3))
        small = pools.enter_context(tc.tile_pool(name="small", bufs=4))
        products = pools.enter_context(tc.tile_pool(name="products", bufs=2 * TILES))
        outgoing = pools.enter_context(tc.tile_pool(name="outgoing", bufs=5))
        psum = pools.enter_context(tc.psum_pool(name="psum", bufs=2))

        identity = const.tile([P, P], F32)
        make_identity(nc, identity[:])
        head_mask = const.tile([P, BATCHES, GROUP_HEADS], F32)
        for b in range(BATCHES):
            nc.vector.tensor_reduce(
                out=head_mask[:, b, :],
                in_=identity[:].rearrange("p (h e) -> p h e", e=HEAD_ROWS),
                axis=mybir.AxisListType.X,
                op=ALU.add,
            )
        k_sum_columns = []
        for i in range(COLUMN_TILES):
            columns = const.tile([P, P], F32, name="k_sum_columns_%d" % i)
            nc.vector.memset(columns[:], 0.0)
            k_sum_columns.append(columns)
        warm = const.tile([P, 2], F32)
        nc.vector.memset(warm[:], 0.0)
        nc.scalar.activation(out=warm[:, 1:2], in_=warm[:, 0:1], func=ACT.Exp)

        x_raw = {}

        def load_x(half):
            for pair in range(TILES // 2):
                first = half * BANK + pair * 2 * P
                raw = keep.tile([P, 2, HIDDEN], BF16, name="x_raw_%d_%d" % (half, pair))
                nc.sync.dma_start(
                    out=raw[:],
                    in_=x_dram[first : first + 2 * P, :].rearrange("(i p) k -> p i k", p=P),
                )
                x_raw[(half, pair)] = raw

        w_raw = {}

        def load_w(w, group):
            for g in range(PASSES):
                raw = keep.tile([P, PACK, BANK], BF16, name="w_raw_%s_%d_%d" % (w, group, g))
                nc.sync.dma_start(
                    out=raw[:],
                    in_=weight_dram[w][
                        g * K_PASS : (g + 1) * K_PASS, group * BANK : (group + 1) * BANK
                    ].rearrange("(p j) n -> p j n", j=PACK),
                )
                w_raw[(w, group, g)] = raw

        later_operands = [("x", 1), ("v", 0), ("q", 1), ("k", 1), ("v", 1)]
        load_x(0)
        load_w("q", 0)
        load_w("k", 0)
        for name, index in later_operands:
            if name == "x":
                load_x(index)
            else:
                load_w(name, index)

        x_grouped = {}
        x_codes = {}
        x_scales = {}

        def turn_x(half):
            grouped = keep.tile([P, PASSES * BANK * PACK], BF16, name="x_grouped_%d" % half, align_bytes=64)
            grouped_words = grouped[:].bitcast(F32).rearrange("p (g r u) -> p g r u", g=PASSES, u=2)
            for i in range(TILES):
                words = x_raw[(half, i // 2)][:, i % 2, :].bitcast(F32).rearrange(
                    "p (g w u) -> p g u w", g=PASSES, u=2
                )
                turned = psum.tile([P, PASSES, 2, P], F32, tag="v")
                for g in range(PASSES):
                    for u in range(2):
                        nc.tensor.transpose(
                            out=turned[:, g, u, :], in_=words[:, g, u, :], identity=identity[:]
                        )
                (nc.scalar.copy if half == 0 else nc.vector.tensor_copy)(
                    out=grouped_words[:, :, i * P : (i + 1) * P, :],
                    in_=turned[:].rearrange("p g u r -> p g r u"),
                )
            x_grouped[half] = grouped

        def quantise_x(half):
            codes = keep.tile([P, PASSES, BANK], U32, name="x_codes_%d" % half, align_bytes=64)
            scales = keep.tile([P, PASSES, BANK], U8, name="x_scales_%d" % half, align_bytes=64)
            nc.vector.quantize_mx(
                out=codes[:].rearrange("p g n -> p (g n)").bitcast(FP8X4),
                scales=scales[:].rearrange("p g n -> p (g n)"),
                in_=x_grouped[half][:],
            )
            x_codes[half] = codes
            x_scales[half] = scales

        w_grouped = {}
        w_codes = {}
        w_scales = {}

        def regroup_w(w, group):
            order = "p (c i) t -> p c t i" if w == "v" else "p (i c) t -> p c t i"
            tag = "w_grouped_first" if (w, group) == ("q", 0) else "w_grouped"
            grouped = stage.tile([P, PASSES, BANK, PACK], BF16, tag=tag, name="w_grouped_%s_%d" % (w, group), bufs=1, align_bytes=64)
            for g, engine_copy in ((0, nc.scalar.copy), (1, nc.vector.tensor_copy)):
                engine_copy(
                    out=grouped[:, g, :, :].rearrange(order, i=4),
                    in_=w_raw[(w, group, g)][:].rearrange("p t (c i) -> p c t i", i=4),
                )
            w_grouped[(w, group)] = grouped

        def quantise_w(w, group):
            codes = keep.tile([P, PASSES, BANK], U32, name="w_codes_%s_%d" % (w, group), align_bytes=64)
            scales = keep.tile([P, PASSES, BANK], U8, name="w_scales_%s_%d" % (w, group), align_bytes=64)
            nc.vector.quantize_mx(
                out=codes[:].rearrange("p g n -> p (g n)").bitcast(FP8X4),
                scales=scales[:].rearrange("p g n -> p (g n)"),
                in_=w_grouped[(w, group)][:].rearrange("p g n t -> p (g n t)"),
            )
            w_codes[(w, group)] = codes
            w_scales[(w, group)] = scales

        def prepare(name, index):
            if name == "x":
                turn_x(index)
                quantise_x(index)
            else:
                regroup_w(name, index)
                quantise_w(name, index)

        def place(number):
            block, tile_in_block = divmod(number, TILES)
            group, half = divmod(block, HALVES)
            return group, half, tile_in_block

        a_banks = {}
        c_banks = {}

        def project(r, w, banks, tag):
            if r >= ROUNDS:
                return
            group, half, t = place(r)
            acc = psum.tile([P, BANK], F32, tag=tag)
            for g in range(PASSES):
                nc.tensor.matmul_mx(
                    out=acc[:],
                    lhsT=w_codes[(w, group)][:, g, t * P : (t + 1) * P].bitcast(FP8X4),
                    lhsT_scale=w_scales[(w, group)][:, g, t * P : (t + 1) * P],
                    rhs=x_codes[half][:, g, :].bitcast(FP8X4),
                    rhs_scale=x_scales[half][:, g, :],
                    start=(g == 0),
                    stop=(g == PASSES - 1),
                )
            banks[r] = acc

        q_tiles = {}
        k_tiles = {}
        k_sums = {}

        def feature_map(r):
            a = a_banks[r]
            c = c_banks[r]
            minus_a = work.tile([P, BANK], F32)
            minus_c = work.tile([P, BANK], F32)
            small_a = work.tile([P, BANK], F32)
            small_c = work.tile([P, BANK], F32)
            nc.scalar.activation(out=minus_a[:], in_=a[:], func=ACT.Relu, scale=-1.0)
            nc.scalar.activation(out=minus_c[:], in_=c[:], func=ACT.Relu, scale=-1.0)
            nc.scalar.activation(out=small_a[:], in_=minus_a[:], func=ACT.Exp, scale=-1.0)
            nc.scalar.activation(out=small_c[:], in_=minus_c[:], func=ACT.Exp, scale=-1.0)
            q = work.tile([P, BANK], F32)
            k = work.tile([P, BANK], F32)
            k_sum = small.tile([P, BATCHES], F32)
            nc.vector.scalar_tensor_tensor(
                out=q[:], in0=a[:], scalar=0.0, in1=small_a[:], op0=ALU.max, op1=ALU.add
            )
            for b in range(BATCHES):
                cols = slice(b * SEQ, (b + 1) * SEQ)
                nc.vector.scalar_tensor_tensor(
                    out=k[:, cols],
                    in0=c[:, cols],
                    scalar=0.0,
                    in1=small_c[:, cols],
                    op0=ALU.max,
                    op1=ALU.add,
                    accum_out=k_sum[:, b : b + 1],
                )
            if r // TILES < MATMUL_BLOCKS:
                nc.vector.tensor_tensor(
                    out=k_sum_columns[r % COLUMN_TILES][:, 0 : BATCHES * GROUP_HEADS].rearrange("p (b h) -> p b h", b=BATCHES),
                    in0=head_mask[:],
                    in1=k_sum[:].unsqueeze(2).to_broadcast([P, BATCHES, GROUP_HEADS]),
                    op=ALU.mult,
                )
            q_tiles[r] = q
            k_tiles[r] = k
            k_sums[r] = k_sum

        qk_tiles = {}
        qs_tiles = {}

        def form_products(r):
            if r // TILES >= MATMUL_BLOCKS:
                qs = products.tile([P, BANK], F32)
                for b in range(BATCHES):
                    cols = slice(b * SEQ, (b + 1) * SEQ)
                    nc.scalar.activation(
                        out=qs[:, cols],
                        in_=q_tiles[r][:, cols],
                        func=ACT.Copy,
                        scale=k_sums[r][:, b : b + 1],
                        bias=NORM_EPS / HEAD,
                    )
                qs_tiles[r] = qs
            qk = products.tile([P, BANK], F32)
            nc.vector.tensor_tensor(out=qk[:], in0=q_tiles[r][:], in1=k_tiles[r][:], op=ALU.mult)
            qk_tiles[r] = qk

        norm_banks = {}
        inverses = {}

        def add_normalizer(r):
            if r >= MATMUL_BLOCKS * TILES:
                return
            block, t = divmod(r, TILES)
            if t == 0:
                norm_banks[block] = psum.tile([P, BANK], F32, tag="sum_qs", name="sum_qs", bufs=1)
            nc.tensor.matmul(
                out=norm_banks[block][:],
                lhsT=k_sum_columns[r % COLUMN_TILES][:],
                rhs=q_tiles[r][:],
                start=(t == 0),
                stop=(t == TILES - 1),
            )

        def turn_normalizer(block):
            rows = work.tile([P, BANK], F32, name="norm_rows")
            nc.scalar.activation(out=rows[:], in_=norm_banks[block][:], func=ACT.Copy, bias=NORM_EPS)
            turned = psum.tile([P, TILES, P], F32, tag="v", name="v")
            for s in range(TILES):
                nc.tensor.transpose(out=turned[:, s, :], in_=rows[:, s * P : (s + 1) * P], identity=identity[:])
            inverse = small.tile([P, TILES, GROUP_HEADS], F32)
            per_batch = TILES // BATCHES
            for b in range(BATCHES):
                nc.vector.reciprocal(
                    out=inverse[:, b * per_batch : (b + 1) * per_batch, :],
                    in_=turned[:, b * per_batch : (b + 1) * per_batch, b * GROUP_HEADS : (b + 1) * GROUP_HEADS],
                )
            inverses[block] = inverse

        block_sums = {}

        def head_sums(block, first=0, last=TILES, late=False):
            for kind, tiles, late_tag in (("qs", qs_tiles, "a"), ("qk", qk_tiles, "c")):
                if kind == "qs" and block < MATMUL_BLOCKS:
                    continue
                if late:
                    turned = psum.tile([P, TILES, P], F32, tag=late_tag, name=late_tag)
                else:
                    turned = psum.tile([P, TILES, P], F32, tag="sum_" + kind, name="sum_" + kind, bufs=1)
                for s in range(TILES):
                    for t in range(first, last):
                        nc.tensor.matmul(
                            out=turned[:, s, :],
                            lhsT=tiles[block * TILES + t][:, s * P : (s + 1) * P],
                            rhs=identity[:],
                            is_transpose=True,
                            start=(t == first),
                            stop=(t == last - 1),
                        )
                block_sums[(kind, block, late)] = turned

        ratios = {}

        early_totals = {}

        def reduce_sums(kind, block, late):
            total = small.tile([P, TILES * GROUP_HEADS], F32, name="total_%s_%d" % (kind, late))
            nc.vector.tensor_reduce(
                out=total[:],
                in_=block_sums[(kind, block, late)][:].rearrange("p s (h e) -> p (s h) e", e=HEAD_ROWS),
                axis=mybir.AxisListType.X,
                op=ALU.add,
            )
            return total

        def form_ratio(block):
            split = block == LAST_BLOCK
            totals = {}
            for kind in ("qs", "qk") if block >= MATMUL_BLOCKS else ("qk",):
                totals[kind] = reduce_sums(kind, block, split)
            ratio = small.tile([P, TILES, GROUP_HEADS], F32)
            if split:
                for kind in ("qs", "qk"):
                    whole = small.tile([P, TILES * GROUP_HEADS], F32, name="whole_" + kind)
                    nc.vector.tensor_tensor(out=whole[:], in0=totals[kind][:], in1=early_totals[kind][:], op=ALU.add)
                    totals[kind] = whole
            if block >= MATMUL_BLOCKS:
                inverse = small.tile([P, TILES, GROUP_HEADS], F32)
                nc.vector.reciprocal(out=inverse[:].rearrange("p s h -> p (s h)"), in_=totals["qs"][:])
                inverses[block] = inverse
            nc.vector.tensor_tensor(
                out=ratio[:].rearrange("p s h -> p (s h)"),
                in0=totals["qk"][:],
                in1=inverses[block][:].rearrange("p s h -> p (s h)"),
                op=ALU.mult,
            )
            ratios[block] = ratio

        v_banks = {}

        def by_scalar(j):
            return j + TILES + SUMS_LAG >= ROUNDS and (j < ROUNDS - TILES or j % 2 == 1)

        def project_value(j):
            if not 0 <= j < ROUNDS:
                return
            group, half, s = place(j)
            tag = ("a" if j in (ROUNDS - 6, ROUNDS - 3) else "c") if by_scalar(j) else "v"
            v = psum.tile([P, BANK], F32, tag=tag, name=tag)
            for g in range(PASSES):
                nc.tensor.matmul_mx(
                    out=v[:],
                    lhsT=x_codes[half][:, g, s * P : (s + 1) * P].bitcast(FP8X4),
                    lhsT_scale=x_scales[half][:, g, s * P : (s + 1) * P],
                    rhs=w_codes[("v", group)][:, g, :].bitcast(FP8X4),
                    rhs_scale=w_scales[("v", group)][:, g, :],
                    start=(g == 0),
                    stop=(g == PASSES - 1),
                )
            v_banks[j] = v

        def scale_and_store(j):
            if j < 0:
                return
            group, half, s = place(j)
            if s == 0:
                form_ratio(j // TILES)
            z = outgoing.tile([P, BANK], F32)
            if by_scalar(j):
                for h in range(GROUP_HEADS):
                    cols = slice(h * HEAD, (h + 1) * HEAD)
                    nc.scalar.activation(
                        out=z[:, cols], in_=v_banks[j][:, cols], func=ACT.Copy, scale=ratios[j // TILES][:, s, h : h + 1]
                    )
            else:
                nc.vector.tensor_tensor(
                    out=z[:].rearrange("p (h d) -> p h d", d=HEAD),
                    in0=v_banks[j][:].rearrange("p (h d) -> p h d", d=HEAD),
                    in1=ratios[j // TILES][:, s, :].unsqueeze(2).to_broadcast([P, GROUP_HEADS, HEAD]),
                    op=ALU.mult,
                )
            first = half * BANK + s * P
            nc.sync.dma_start(
                out=out_dram[first : first + P, group * BANK : (group + 1) * BANK], in_=z[:]
            )

        with tc.manual_schedule(engines={mybir.EngineType.PE, mybir.EngineType.Activation, mybir.EngineType.DVE}):
            turn_x(0)
            regroup_w("q", 0)
            quantise_x(0)
            regroup_w("k", 0)
            quantise_w("q", 0)
            for r in range(AHEAD):
                project(r, "q", a_banks, "a")
            quantise_w("k", 0)
            for r in range(AHEAD):
                project(r, "k", c_banks, "c")
            prepare(later_operands[0][0], later_operands[0][1])
        for r in range(ROUNDS + SUMS_LAG + 1):
            if r < ROUNDS:
                feature_map(r)
                form_products(r)
            scale_and_store(r - TILES - SUMS_LAG)
            if r % TILES == 0 and 1 <= r // TILES <= MATMUL_BLOCKS:
                turn_normalizer(r // TILES - 1)
            if 2 <= r <= len(later_operands):
                prepare(later_operands[r - 1][0], later_operands[r - 1][1])
            if r == ROUNDS:
                for kind in ("qs", "qk"):
                    early_totals[kind] = reduce_sums(kind, LAST_BLOCK, False)
            if r == ROUNDS - 1:
                head_sums(LAST_BLOCK, 0, TILES - 1)
            if r >= TILES + SUMS_LAG - 1 and (r - SUMS_LAG + 1) % TILES == 0:
                block = (r - SUMS_LAG + 1) // TILES - 1
                if block == LAST_BLOCK:
                    head_sums(block, TILES - 1, TILES, late=True)
                else:
                    head_sums(block)
            project(r + AHEAD, "q", a_banks, "a")
            project(r + AHEAD, "k", c_banks, "c")
            project_value(r - TILES - SUMS_LAG + 1)
            add_normalizer(r)
        for j in range(ROUNDS - TILES + 1, ROUNDS):
            project_value(j + 1)
            scale_and_store(j)
